import numpy as np
import ml_dtypes


def mxq(x, axis, fmt="e4m3"):
    dtype, down = {"e4m3": (ml_dtypes.float8_e4m3fn, 7), "e5m2": (ml_dtypes.float8_e5m2, 14)}[fmt]
    v = np.moveaxis(np.asarray(x, np.float32).astype(ml_dtypes.bfloat16).astype(np.float64), axis, -1)
    blocks = v.reshape(v.shape[:-1] + (-1, 32))
    amax = np.abs(blocks).max(-1, keepdims=True)
    byte = np.maximum(np.where(amax > 0, np.frexp(amax)[1] - 1 + 127, 0) - down, 1)
    scale = np.exp2(byte - 127.0)
    codes = (blocks / scale).astype(np.float32).astype(dtype).astype(np.float64)
    return np.moveaxis((codes * scale).reshape(v.shape), -1, axis)


WIDE = False


def mx_kscale(k):
    if not WIDE:
        return np.ones(k)
    levels = np.array([10, -10, 5, -5, 0])
    a = np.random.permutation(np.resize(levels, k // 512 * 4)).reshape(k // 512, 4)
    idx = np.arange(k)
    return np.exp2(a[idx // 512, idx % 128 // 32])


BF16 = ml_dtypes.bfloat16


def bf(x):
    return np.asarray(x, np.float32).astype(BF16)


def f64(x):
    return np.asarray(x).astype(np.float64)


E2M1 = np.array([0.0, 0.5, 1.0, 1.5, 2.0, 3.0, 4.0, 6.0, -0.0, -0.5, -1.0, -1.5, -2.0, -3.0, -4.0, -6.0])


def pack_weight(w, fmt):
    k, n = w.shape
    w = f64(bf(w)).reshape(k // 32, 32, n)
    amax = np.abs(w).max(1)
    if fmt == "e4m3":
        byte = np.frexp(amax)[1] - 1 + 127 - 7
    else:
        mant, ex = np.frexp(amax / 6.0)
        byte = np.where(mant > 0.5, ex, ex - 1) + 127
    byte = np.clip(np.where(amax > 0, byte, 1), 1, 254)
    scaled = (w * np.exp2(127.0 - byte)[:, None, :]).reshape(k, n).astype(np.float32)
    by_word = np.ascontiguousarray(scaled.reshape(k // 512, 128, 4, n).transpose(0, 1, 3, 2))
    if fmt == "e4m3":
        words = by_word.astype(ml_dtypes.float8_e4m3fn).view(np.uint8)
    else:
        c = by_word.astype(ml_dtypes.float4_e2m1fn).view(np.uint8) & 0xF
        words = c[..., 0::2] | (c[..., 1::2] << 4)
    return np.ascontiguousarray(words), np.ascontiguousarray(byte.astype(np.uint8).reshape(k // 512, 16, n))


def unpack_weight(words, scales, fmt):
    g, p, n, _ = words.shape
    if fmt == "e4m3":
        vals = np.ascontiguousarray(words).view(ml_dtypes.float8_e4m3fn).astype(np.float64)
    else:
        nib = np.empty((g, p, n, 4), np.uint8)
        nib[..., 0::2] = words & 0xF
        nib[..., 1::2] = words >> 4
        vals = E2M1[nib]
    vals = vals * np.repeat(np.exp2(scales.astype(np.float64) - 127.0), 8, axis=1)[..., None]
    return vals.transpose(0, 1, 3, 2).reshape(g * 512, n)


B, F, H, E = 128, 2, 4096, 2048


def setup_inputs():
    t = mx_kscale(H)
    x = bf(np.random.standard_normal((B, F)))
    w1 = bf(np.random.uniform(-1.0, 1.0, (F, H)) * t)
    b1 = bf(np.random.uniform(-1.0, 1.0, (F, H)) * t)
    w2 = np.random.standard_normal((F, H, E)) * 1.5 / np.sqrt(H) / t[None, :, None]
    w2_words, w2_scales = pack_weight(w2.reshape(-1, E), "e4m3")
    b2 = bf(np.random.standard_normal((F, E)) * 0.3)
    return {"x": x,
            "w1": w1,
            "b1": b1,
            "w2_words": w2_words,
            "w2_scales": w2_scales,
            "b2": b2}


def reference(x, w1, b1, w2_words, w2_scales, b2):
    h = np.maximum(f64(x)[:, :, None] * f64(w1)[None] + f64(b1)[None], 0.0)
    hq = mxq(h, 2, "e4m3")
    out = (hq.transpose(1, 0, 2) @ unpack_weight(w2_words, w2_scales, "e4m3").reshape(F, H, E)).transpose(1, 0, 2) + f64(b2)[None]
    return out.reshape(x.shape[0], F * E)

@@ -1,0 +1,171 @@
+from contextlib import ExitStack
+
+import concourse.mybir as mybir
+from concourse.masks import make_identity
+
+BF16 = mybir.dt.bfloat16
+F32 = mybir.dt.float32
+I32 = mybir.dt.int32
+U8 = mybir.dt.uint8
+FP8X4 = mybir.dt.float8_e4m3fn_x4
+
+P = 128
+B, F, H, E = 128, 2, 4096, 2048
+PACK = 4
+K_PASS = P * PACK
+GROUPS_PER_FEATURE = H // K_PASS
+GROUPS = F * GROUPS_PER_FEATURE
+N_TILE = 512
+N_TILES = E // N_TILE
+QUAD = 4
+SCALE_ROWS = 4
+AHEAD = 2
+
+FLOPS = 2 * B * F * H * E
+
+
+def tile_densefeaturenumericembedding_w_e_kernel(
+    tc, x, w1, b1, w2_words, w2_scales, b2, out
+):
+    nc = tc.nc
+    with ExitStack() as ctx:
+        keep = ctx.enter_context(tc.tile_pool(name="keep", bufs=1))
+        stage = ctx.enter_context(tc.tile_pool(name="stage", bufs=4))
+        psum_plain = ctx.enter_context(tc.psum_pool(name="psum_plain", bufs=2))
+        psum_acc = ctx.enter_context(tc.psum_pool(name="psum_acc", bufs=N_TILES))
+
+        words = [keep.tile([P, E], I32, name="words%d" % g, align_bytes=64) for g in range(GROUPS)]
+        planes = [keep.tile([P, E], U8, name="planes%d" % q, align_bytes=64) for q in range(GROUPS // QUAD)]
+
+        def load_scales(q):
+            nc.vector.memset(planes[q][:].bitcast(I32), 0)
+            for quadrant in range(P // 32):
+                nc.sync.dma_start(
+                    out=planes[q][32 * quadrant : 32 * quadrant + QUAD * SCALE_ROWS, :].bitcast(I32),
+                    in_=w2_scales[
+                        QUAD * q : QUAD * (q + 1), SCALE_ROWS * quadrant : SCALE_ROWS * (quadrant + 1), :
+                    ].bitcast(I32),
+                )
+
+        def load_words(g, pieces):
+            width = E // pieces
+            for piece in range(pieces):
+                cols = slice(piece * width, (piece + 1) * width)
+                nc.sync.dma_start(
+                    out=words[g][:, cols],
+                    in_=w2_words[g, :, cols, :].rearrange("p n t -> p (n t)").bitcast(I32),
+                )
+
+        x_flat = keep.tile([F, B * F], BF16)
+        nc.sync.dma_start(out=x_flat[:], in_=x.rearrange("b f -> (b f)").partition_broadcast(F))
+        wb_loaded = keep.tile([2 * F, H], BF16)
+        nc.sync.dma_start(out=wb_loaded[0:F, :], in_=w1)
+        nc.sync.dma_start(out=wb_loaded[F : 2 * F, :], in_=b1)
+
+        b2_rows = keep.tile([P, N_TILE], BF16)
+        nc.vector.memset(b2_rows[:], 0.0)
+
+        for g in range(GROUPS):
+            if g % QUAD == 0:
+                load_scales(g // QUAD)
+            load_words(g, N_TILES if g == GROUPS - 1 else 1)
+            if g == 1:
+                nc.sync.dma_start(
+                    out=b2_rows[0 : F * N_TILES, :], in_=b2.rearrange("f (c n) -> (f c) n", n=N_TILE)
+                )
+
+        ident = keep.tile([P, P], BF16)
+        make_identity(nc, ident[:])
+
+        wb_rows = keep.tile([P, GROUPS_PER_FEATURE, PACK, P], BF16)
+        nc.vector.memset(wb_rows[:].rearrange("r g t p -> r (g t p)").bitcast(I32), 0)
+
+        x_rows = keep.tile([P, F, B], BF16)
+        nc.vector.tensor_copy(out=x_rows[:], in_=ident[:, F : 2 * F].unsqueeze(2).to_broadcast([P, F, B]))
+        nc.vector.tensor_tensor(
+            out=x_rows[0:F],
+            in0=x_flat[:].rearrange("r (b f) -> r f b", f=F),
+            in1=ident[0:F, 0:F].unsqueeze(2).to_broadcast([F, F, B]),
+            op=mybir.AluOpType.mult,
+        )
+
+        h_codes = keep.tile([P, GROUPS, B], I32, align_bytes=64)
+        h_scales = keep.tile([P, GROUPS, B], U8, align_bytes=64)
+
+        def make_hidden(g):
+            f, group_of_f = divmod(g, GROUPS_PER_FEATURE)
+            if f == 0:
+                nc.vector.tensor_copy(
+                    out=wb_rows[0 : 2 * F, group_of_f],
+                    in_=wb_loaded[:, K_PASS * group_of_f : K_PASS * (group_of_f + 1)].rearrange(
+                        "r (p t) -> r t p", t=PACK
+                    ),
+                )
+            pre = psum_plain.tile([P, PACK, B], F32)
+            for t in range(PACK):
+                nc.tensor.matmul(
+                    out=pre[:, t, :],
+                    lhsT=wb_rows[:, group_of_f, t, :],
+                    rhs=x_rows[:, f, :],
+                    start=True,
+                    stop=True,
+                )
+            h_bf = stage.tile([P, B, PACK], BF16, align_bytes=64)
+            side_by_side = pre[:].rearrange("p t b -> p b t")
+            if g % 2 == 0:
+                nc.vector.tensor_scalar_max(out=h_bf[:], in0=side_by_side, scalar1=0.0)
+            else:
+                nc.scalar.activation(
+                    out=h_bf[:], in_=side_by_side, func=mybir.ActivationFunctionType.Relu
+                )
+            nc.vector.quantize_mx(
+                out=h_codes[:, g, :].bitcast(FP8X4),
+                scales=h_scales[:, g, :],
+                in_=h_bf[:].rearrange("p b t -> p (b t)"),
+            )
+
+        result = [keep.tile([P, E], F32, name="result%d" % f) for f in range(F)]
+
+        def spread_bias(f):
+            for nt in range(N_TILES):
+                row = f * N_TILES + nt
+                bias_ps = psum_plain.tile([P, N_TILE], F32)
+                nc.tensor.matmul(
+                    out=bias_ps[:],
+                    lhsT=ident[:, row : row + 1].to_broadcast([P, P]),
+                    rhs=b2_rows[:],
+                    start=True,
+                    stop=True,
+                )
+                nc.scalar.copy(out=result[f][:, nt * N_TILE : (nt + 1) * N_TILE], in_=bias_ps[:])
+
+        for g in range(AHEAD):
+            make_hidden(g)
+        for f in range(F):
+            acc = [psum_acc.tile([P, N_TILE], F32, name="acc%d" % nt, tag="acc") for nt in range(N_TILES)]
+            for group_of_f in range(GROUPS_PER_FEATURE):
+                g = f * GROUPS_PER_FEATURE + group_of_f
+                if g + AHEAD < GROUPS:
+                    make_hidden(g + AHEAD)
+                if group_of_f == GROUPS_PER_FEATURE // 2:
+                    spread_bias(f)
+                offset = SCALE_ROWS * (g % QUAD)
+                for nt in range(N_TILES):
+                    cols = slice(nt * N_TILE, (nt + 1) * N_TILE)
+                    nc.tensor.matmul_mx(
+                        out=acc[nt][:],
+                        lhsT=h_codes[:, g, :].bitcast(FP8X4),
+                        lhsT_scale=h_scales[:, g, :],
+                        rhs=words[g][:, cols].bitcast(FP8X4),
+                        rhs_scale=planes[g // QUAD][offset:P, cols],
+                        start=(group_of_f == 0),
+                        stop=(group_of_f == GROUPS_PER_FEATURE - 1),
+                    )
+            for nt in range(N_TILES):
+                cols = slice(nt * N_TILE, (nt + 1) * N_TILE)
+                nc.vector.tensor_tensor(
+                    out=result[f][:, cols], in0=acc[nt][:], in1=result[f][:, cols], op=mybir.AluOpType.add
+                )
+                nc.scalar.dma_start(
+                    out=out[:, f * E + nt * N_TILE : f * E + (nt + 1) * N_TILE], in_=result[f][:, cols]
+                )

@@ -65,9 +65,9 @@ def tile_densefeaturenumericembedding_w_e_kernel(
         b2_rows = keep.tile([P, N_TILE], BF16)
         nc.vector.memset(b2_rows[:], 0.0)
 
+        for q in range(GROUPS // QUAD):
+            load_scales(q)
         for g in range(GROUPS):
-            if g % QUAD == 0:
-                load_scales(g // QUAD)
             load_words(g, N_TILES if g == GROUPS - 1 else 1)
             if g == 1:
                 nc.sync.dma_start(

@@ -166,6 +166,6 @@ def tile_densefeaturenumericembedding_w_e_kernel(
                 nc.vector.tensor_tensor(
                     out=result[f][:, cols], in0=acc[nt][:], in1=result[f][:, cols], op=mybir.AluOpType.add
                 )
-                nc.scalar.dma_start(
+                nc.sync.dma_start(
                     out=out[:, f * E + nt * N_TILE : f * E + (nt + 1) * N_TILE], in_=result[f][:, cols]
                 )

@@ -20,6 +20,7 @@ N_TILES = E // N_TILE
 QUAD = 4
 SCALE_ROWS = 4
 AHEAD = 2
+PAIRED = 10
 
 FLOPS = 2 * B * F * H * E
 
@@ -34,7 +35,12 @@ def tile_densefeaturenumericembedding_w_e_kernel(
         psum_plain = ctx.enter_context(tc.psum_pool(name="psum_plain", bufs=2))
         psum_acc = ctx.enter_context(tc.psum_pool(name="psum_acc", bufs=N_TILES))
 
-        words = [keep.tile([P, E], I32, name="words%d" % g, align_bytes=64) for g in range(GROUPS)]
+        pairs = [keep.tile([P, 2, E], I32, name="pair%d" % i, align_bytes=64) for i in range(PAIRED // 2)]
+        singles = [keep.tile([P, E], I32, name="words%d" % g, align_bytes=64) for g in range(PAIRED, GROUPS)]
+
+        def words_of(g, cols):
+            return pairs[g // 2][:, g % 2, cols] if g < PAIRED else singles[g - PAIRED][:, cols]
+
         planes = [keep.tile([P, E], U8, name="planes%d" % q, align_bytes=64) for q in range(GROUPS // QUAD)]
 
         def load_scales(q):
@@ -52,9 +58,15 @@ def tile_densefeaturenumericembedding_w_e_kernel(
             for piece in range(pieces):
                 cols = slice(piece * width, (piece + 1) * width)
                 nc.sync.dma_start(
-                    out=words[g][:, cols],
+                    out=words_of(g, cols),
                     in_=w2_words[g, :, cols, :].rearrange("p n t -> p (n t)").bitcast(I32),
                 )
+
+        def load_pair(i):
+            nc.sync.dma_start(
+                out=pairs[i][:],
+                in_=w2_words[2 * i : 2 * i + 2].rearrange("g p n t -> p g (n t)").bitcast(I32),
+            )
 
         x_flat = keep.tile([F, B * F], BF16)
         nc.sync.dma_start(out=x_flat[:], in_=x.rearrange("b f -> (b f)").partition_broadcast(F))
@@ -68,7 +80,10 @@ def tile_densefeaturenumericembedding_w_e_kernel(
         for q in range(GROUPS // QUAD):
             load_scales(q)
         for g in range(GROUPS):
-            load_words(g, N_TILES if g == GROUPS - 1 else 1)
+            if g >= PAIRED:
+                load_words(g, N_TILES if g == GROUPS - 1 else 1)
+            elif g % 2 == 0:
+                load_pair(g // 2)
             if g == 1:
                 nc.sync.dma_start(
                     out=b2_rows[0 : F * N_TILES, :], in_=b2.rearrange("f (c n) -> (f c) n", n=N_TILE)
@@ -156,16 +171,19 @@ def tile_densefeaturenumericembedding_w_e_kernel(
                         out=acc[nt][:],
                         lhsT=h_codes[:, g, :].bitcast(FP8X4),
                         lhsT_scale=h_scales[:, g, :],
-                        rhs=words[g][:, cols].bitcast(FP8X4),
+                        rhs=words_of(g, cols).bitcast(FP8X4),
                         rhs_scale=planes[g // QUAD][offset:P, cols],
                         start=(group_of_f == 0),
                         stop=(group_of_f == GROUPS_PER_FEATURE - 1),
                     )
+            banks_per_store = N_TILES if f < F - 1 else 1
             for nt in range(N_TILES):
                 cols = slice(nt * N_TILE, (nt + 1) * N_TILE)
                 nc.vector.tensor_tensor(
                     out=result[f][:, cols], in0=acc[nt][:], in1=result[f][:, cols], op=mybir.AluOpType.add
                 )
-                nc.sync.dma_start(
-                    out=out[:, f * E + nt * N_TILE : f * E + (nt + 1) * N_TILE], in_=result[f][:, cols]
-                )
+                if (nt + 1) % banks_per_store == 0:
+                    done = slice((nt + 1 - banks_per_store) * N_TILE, (nt + 1) * N_TILE)
+                    nc.sync.dma_start(
+                        out=out[:, f * E + done.start : f * E + done.stop], in_=result[f][:, done]
+                    )

from contextlib import ExitStack

import concourse.mybir as mybir
from concourse.masks import make_identity

BF16 = mybir.dt.bfloat16
F32 = mybir.dt.float32
I32 = mybir.dt.int32
U8 = mybir.dt.uint8
FP8X4 = mybir.dt.float8_e4m3fn_x4

P = 128
B, F, H, E = 128, 2, 4096, 2048
PACK = 4
K_PASS = P * PACK
GROUPS_PER_FEATURE = H // K_PASS
GROUPS = F * GROUPS_PER_FEATURE
N_TILE = 512
N_TILES = E // N_TILE
QUAD = 4
SCALE_ROWS = 4
AHEAD = 2
PAIRED = 10

FLOPS = 2 * B * F * H * E


def tile_densefeaturenumericembedding_w_e_kernel(
    tc, x, w1, b1, w2_words, w2_scales, b2, out
):
    nc = tc.nc
    with ExitStack() as ctx:
        keep = ctx.enter_context(tc.tile_pool(name="keep", bufs=1))
        stage = ctx.enter_context(tc.tile_pool(name="stage", bufs=4))
        psum_plain = ctx.enter_context(tc.psum_pool(name="psum_plain", bufs=2))
        psum_acc = ctx.enter_context(tc.psum_pool(name="psum_acc", bufs=N_TILES))

        pairs = [keep.tile([P, 2, E], I32, name="pair%d" % i, align_bytes=64) for i in range(PAIRED // 2)]
        singles = [keep.tile([P, E], I32, name="words%d" % g, align_bytes=64) for g in range(PAIRED, GROUPS)]

        def words_of(g, cols):
            return pairs[g // 2][:, g % 2, cols] if g < PAIRED else singles[g - PAIRED][:, cols]

        planes = [keep.tile([P, E], U8, name="planes%d" % q, align_bytes=64) for q in range(GROUPS // QUAD)]

        def load_scales(q):
            nc.vector.memset(planes[q][:].bitcast(I32), 0)
            for quadrant in range(P // 32):
                nc.sync.dma_start(
                    out=planes[q][32 * quadrant : 32 * quadrant + QUAD * SCALE_ROWS, :].bitcast(I32),
                    in_=w2_scales[
                        QUAD * q : QUAD * (q + 1), SCALE_ROWS * quadrant : SCALE_ROWS * (quadrant + 1), :
                    ].bitcast(I32),
                )

        def load_words(g, pieces):
            width = E // pieces
            for piece in range(pieces):
                cols = slice(piece * width, (piece + 1) * width)
                nc.sync.dma_start(
                    out=words_of(g, cols),
                    in_=w2_words[g, :, cols, :].rearrange("p n t -> p (n t)").bitcast(I32),
                )

        def load_pair(i):
            nc.sync.dma_start(
                out=pairs[i][:],
                in_=w2_words[2 * i : 2 * i + 2].rearrange("g p n t -> p g (n t)").bitcast(I32),
            )

        x_flat = keep.tile([F, B * F], BF16)
        nc.sync.dma_start(out=x_flat[:], in_=x.rearrange("b f -> (b f)").partition_broadcast(F))
        wb_loaded = keep.tile([2 * F, H], BF16)
        nc.sync.dma_start(out=wb_loaded[0:F, :], in_=w1)
        nc.sync.dma_start(out=wb_loaded[F : 2 * F, :], in_=b1)

        b2_rows = keep.tile([P, N_TILE], BF16)
        nc.vector.memset(b2_rows[:], 0.0)

        for q in range(GROUPS // QUAD):
            load_scales(q)
        for g in range(GROUPS):
            if g >= PAIRED:
                load_words(g, N_TILES if g == GROUPS - 1 else 1)
            elif g % 2 == 0:
                load_pair(g // 2)
            if g == 1:
                nc.sync.dma_start(
                    out=b2_rows[0 : F * N_TILES, :], in_=b2.rearrange("f (c n) -> (f c) n", n=N_TILE)
                )

        ident = keep.tile([P, P], BF16)
        make_identity(nc, ident[:])

        wb_rows = keep.tile([P, GROUPS_PER_FEATURE, PACK, P], BF16)
        nc.vector.memset(wb_rows[:].rearrange("r g t p -> r (g t p)").bitcast(I32), 0)

        x_rows = keep.tile([P, F, B], BF16)
        nc.vector.tensor_copy(out=x_rows[:], in_=ident[:, F : 2 * F].unsqueeze(2).to_broadcast([P, F, B]))
        nc.vector.tensor_tensor(
            out=x_rows[0:F],
            in0=x_flat[:].rearrange("r (b f) -> r f b", f=F),
            in1=ident[0:F, 0:F].unsqueeze(2).to_broadcast([F, F, B]),
            op=mybir.AluOpType.mult,
        )

        h_codes = keep.tile([P, GROUPS, B], I32, align_bytes=64)
        h_scales = keep.tile([P, GROUPS, B], U8, align_bytes=64)

        def make_hidden(g):
            f, group_of_f = divmod(g, GROUPS_PER_FEATURE)
            if f == 0:
                nc.vector.tensor_copy(
                    out=wb_rows[0 : 2 * F, group_of_f],
                    in_=wb_loaded[:, K_PASS * group_of_f : K_PASS * (group_of_f + 1)].rearrange(
                        "r (p t) -> r t p", t=PACK
                    ),
                )
            pre = psum_plain.tile([P, PACK, B], F32)
            for t in range(PACK):
                nc.tensor.matmul(
                    out=pre[:, t, :],
                    lhsT=wb_rows[:, group_of_f, t, :],
                    rhs=x_rows[:, f, :],
                    start=True,
                    stop=True,
                )
            h_bf = stage.tile([P, B, PACK], BF16, align_bytes=64)
            side_by_side = pre[:].rearrange("p t b -> p b t")
            if g % 2 == 0:
                nc.vector.tensor_scalar_max(out=h_bf[:], in0=side_by_side, scalar1=0.0)
            else:
                nc.scalar.activation(
                    out=h_bf[:], in_=side_by_side, func=mybir.ActivationFunctionType.Relu
                )
            nc.vector.quantize_mx(
                out=h_codes[:, g, :].bitcast(FP8X4),
                scales=h_scales[:, g, :],
                in_=h_bf[:].rearrange("p b t -> p (b t)"),
            )

        result = [keep.tile([P, E], F32, name="result%d" % f) for f in range(F)]

        def spread_bias(f):
            for nt in range(N_TILES):
                row = f * N_TILES + nt
                bias_ps = psum_plain.tile([P, N_TILE], F32)
                nc.tensor.matmul(
                    out=bias_ps[:],
                    lhsT=ident[:, row : row + 1].to_broadcast([P, P]),
                    rhs=b2_rows[:],
                    start=True,
                    stop=True,
                )
                nc.scalar.copy(out=result[f][:, nt * N_TILE : (nt + 1) * N_TILE], in_=bias_ps[:])

        for g in range(AHEAD):
            make_hidden(g)
        for f in range(F):
            acc = [psum_acc.tile([P, N_TILE], F32, name="acc%d" % nt, tag="acc") for nt in range(N_TILES)]
            for group_of_f in range(GROUPS_PER_FEATURE):
                g = f * GROUPS_PER_FEATURE + group_of_f
                if g + AHEAD < GROUPS:
                    make_hidden(g + AHEAD)
                if group_of_f == GROUPS_PER_FEATURE // 2:
                    spread_bias(f)
                offset = SCALE_ROWS * (g % QUAD)
                for nt in range(N_TILES):
                    cols = slice(nt * N_TILE, (nt + 1) * N_TILE)
                    nc.tensor.matmul_mx(
                        out=acc[nt][:],
                        lhsT=h_codes[:, g, :].bitcast(FP8X4),
                        lhsT_scale=h_scales[:, g, :],
                        rhs=words_of(g, cols).bitcast(FP8X4),
                        rhs_scale=planes[g // QUAD][offset:P, cols],
                        start=(group_of_f == 0),
                        stop=(group_of_f == GROUPS_PER_FEATURE - 1),
                    )
            banks_per_store = N_TILES if f < F - 1 else 1
            for nt in range(N_TILES):
                cols = slice(nt * N_TILE, (nt + 1) * N_TILE)
                nc.vector.tensor_tensor(
                    out=result[f][:, cols], in0=acc[nt][:], in1=result[f][:, cols], op=mybir.AluOpType.add
                )
                if (nt + 1) % banks_per_store == 0:
                    done = slice((nt + 1 - banks_per_store) * N_TILE, (nt + 1) * N_TILE)
                    nc.sync.dma_start(
                        out=out[:, f * E + done.start : f * E + done.stop], in_=result[f][:, done]
                    )
